import numpy as np
import ml_dtypes


def mxq(x, axis, fmt="e4m3"):
    dtype, down = {"e4m3": (ml_dtypes.float8_e4m3fn, 7), "e5m2": (ml_dtypes.float8_e5m2, 14)}[fmt]
    v = np.moveaxis(np.asarray(x, np.float32).astype(ml_dtypes.bfloat16).astype(np.float64), axis, -1)
    blocks = v.reshape(v.shape[:-1] + (-1, 32))
    amax = np.abs(blocks).max(-1, keepdims=True)
    byte = np.maximum(np.where(amax > 0, np.frexp(amax)[1] - 1 + 127, 0) - down, 1)
    scale = np.exp2(byte - 127.0)
    codes = (blocks / scale).astype(np.float32).astype(dtype).astype(np.float64)
    return np.moveaxis((codes * scale).reshape(v.shape), -1, axis)


WIDE = False


def mx_kscale(k):
    if not WIDE:
        return np.ones(k)
    levels = np.array([10, -10, 5, -5, 0])
    if k % 512:
        return np.exp2(np.random.permutation(np.resize(levels, k // 32))).repeat(32)
    a = np.empty((k // 512, 16))
    for p in range(k // 512):
        a[p, :8] = np.random.permutation(np.resize(levels, 8))
        for g in range(8):
            far = levels[np.abs(levels - a[p, g]) >= 10]
            a[p, g + 8] = far[np.random.randint(len(far))]
    return np.exp2(a.ravel()).repeat(32)


BF16 = ml_dtypes.bfloat16


def bf(x):
    return np.asarray(x, np.float32).astype(BF16)


def f64(x):
    return np.asarray(x).astype(np.float64)


B, T, C, R, H, DN, DR, DV = 2, 256, 2048, 512, 16, 128, 64, 128
DQ = DN + DR
NF = DR // 2


def rotate_half(u):
    u1, u2 = u[..., : u.shape[-1] // 2], u[..., u.shape[-1] // 2 :]
    return np.concatenate([-u2, u1], axis=-1)


def draw0():
    s, t = mx_kscale(C), mx_kscale(R)
    return {
        "x": bf(np.random.standard_normal((B, T, C)) * s),
        "freqs_cis": bf(np.stack([np.random.uniform(size=(T, NF)), np.random.uniform(size=(T, NF))], axis=-1)),
        "w_kv_down": bf(np.random.standard_normal((C, R)) / np.sqrt(C) / s[:, None] * t),
        "w_k_up": bf(np.random.standard_normal((R, H * DQ)) / np.sqrt(R) / t[:, None]),
        "w_v_up": bf(np.random.standard_normal((R, H * DV)) / np.sqrt(R) / t[:, None]),
    }


def core(x, freqs_cis, w_kv_down, w_k_up, w_v_up):
    kv = mxq(f64(x), 2, "e4m3") @ mxq(f64(w_kv_down), 0, "e4m3")
    kvq = mxq(kv, 2, "e4m3")
    k = (kvq @ mxq(f64(w_k_up), 0, "e4m3")).reshape(B, T, H, DQ)
    v = (kvq @ mxq(f64(w_v_up), 0, "e4m3")).reshape(B, T, H, DV)
    k_nope, k_rope = k[..., :DN], k[..., DN:]
    freqs = f64(freqs_cis)
    cos = freqs[..., 0][None, :, None, :]
    sin = freqs[..., 1][None, :, None, :]
    rep = DR // cos.shape[-1]
    cos = np.tile(cos, (1, 1, 1, rep))
    sin = np.tile(sin, (1, 1, 1, rep))
    k_rope = k_rope * cos + rotate_half(k_rope) * sin
    return np.concatenate([k_nope, k_rope], axis=-1), v


def e4m3fn_bytes(y):
    return np.clip(np.asarray(y, np.float64), -448.0, 448.0).astype(np.float32).astype(ml_dtypes.float8_e4m3fn).view(np.uint8)


def e4m3fn_values(b):
    return np.asarray(b, np.uint8).view(ml_dtypes.float8_e4m3fn).astype(np.float64)


def setup_inputs():
    d = draw0()
    x0 = np.asarray(d['w_k_up']).astype(np.float64)
    s = (np.max(np.abs(x0), axis=(1,), keepdims=True) / 448.0).astype(np.float32)
    out = {}
    for k, v in d.items():
        if k == 'w_k_up':
            out['w_k_up_bytes'] = e4m3fn_bytes(x0 / s.astype(np.float64))
            out['w_k_up_scale'] = s
        else:
            out[k] = v
    return out


def reference(x, freqs_cis, w_kv_down, w_k_up_bytes, w_k_up_scale, w_v_up):
    return core(x, freqs_cis, w_kv_down, e4m3fn_values(w_k_up_bytes) * w_k_up_scale.astype(np.float64), w_v_up)

@@ -1,0 +1,519 @@
+from contextlib import ExitStack
+
+import concourse.mybir as mybir
+from concourse.masks import make_identity
+
+F32 = mybir.dt.float32
+BF16 = mybir.dt.bfloat16
+U32 = mybir.dt.uint32
+U8 = mybir.dt.uint8
+FP8 = mybir.dt.float8_e4m3fn
+FP8X4 = mybir.dt.float8_e4m3fn_x4
+MULT = mybir.AluOpType.mult
+ADD = mybir.AluOpType.add
+COPY = mybir.ActivationFunctionType.Copy
+
+B, T, C, R, H, DN, DR, DV = 2, 256, 2048, 512, 16, 128, 64, 128
+DQ = DN + DR
+HALF = DR // 2
+P = 128
+PACK = 4
+KP = P * PACK
+PASSES = C // KP
+TILES = B * T // P
+BANK = 512
+UH = 8
+UNITS = H // UH
+UW = UH * DQ
+UN = UH * DN
+UR = UH * DR
+VW = 1024
+VUNITS = H * DV // VW
+
+FLOPS = 2 * B * T * C * R + 2 * B * T * R * H * (DQ + DV)
+
+
+def tile_fa3mlaattention_pa_kernel(tc, x, freqs_cis, w_kv_down, w_k_up_bytes, w_k_up_scale, w_v_up, out_0, out_1):
+    nc = tc.nc
+    x_rows = x.rearrange("b t c -> (b t) c")
+    k_rows = out_0.rearrange("b t h d -> (b t) (h d)")
+    v_rows = out_1.rearrange("b t h d -> (b t) (h d)")
+
+    with ExitStack() as ctx:
+        keep = ctx.enter_context(tc.tile_pool(name="keep", bufs=1))
+        work = ctx.enter_context(tc.tile_pool(name="work", bufs=3))
+        outs = ctx.enter_context(tc.tile_pool(name="outs", bufs=4))
+        psum = ctx.enter_context(tc.psum_pool(name="psum", bufs=8))
+
+        wd_raw = keep.tile([P, PASSES, PACK, R], BF16, align_bytes=64)
+        x_raw = keep.tile([P, TILES, C], BF16, align_bytes=64)
+        scale = keep.tile([P, PACK], F32)
+        freqs = keep.tile([P, T // P, HALF, 2], BF16)
+        wk_raw = []
+        wv_raw = []
+        for u in range(UNITS):
+            raw_k = keep.tile([P, PACK, UW], U8, name="wk_raw%d" % u, align_bytes=64)
+            wk_raw.append(raw_k)
+        for u in range(VUNITS):
+            raw_v = keep.tile([P, PACK, VW], BF16, name="wv_raw%d" % u, align_bytes=64)
+            wv_raw.append(raw_v)
+        wd_view = w_kv_down.rearrange("(g p j) n -> g p j n", p=P, j=PACK)
+        wk_view = w_k_up_bytes.rearrange("(p j) n -> p j n", j=PACK)
+        wv_view = w_v_up.rearrange("(p j) n -> p j n", j=PACK)
+
+        def load_wd(g):
+            nc.sync.dma_start(out=wd_raw[:, g], in_=wd_view[g])
+
+        def load_x(i):
+            nc.sync.dma_start(out=x_raw[:, i], in_=x_rows[i * P : (i + 1) * P, :])
+
+        def load_wk(u):
+            nc.sync.dma_start(out=wk_raw[u][:], in_=wk_view[:, :, u * UW : (u + 1) * UW])
+
+        def load_wka(j):
+            nc.sync.dma_start(out=wk_raw[0][:, j, :], in_=wk_view[:, j, 0:UW])
+
+        def load_wv(c):
+            cols = slice(c * BANK, (c + 1) * BANK)
+            nc.sync.dma_start(out=wv_raw[c // 2][:, :, (c % 2) * BANK : (c % 2 + 1) * BANK], in_=wv_view[:, :, cols])
+
+        load_wka(0)
+        load_wka(1)
+        nc.sync.dma_start(out=scale[:], in_=w_k_up_scale.rearrange("(p j) o -> p (j o)", j=PACK))
+        load_wv(0)
+        load_wka(3)
+        load_wd(0)
+        load_wka(2)
+        load_wd(2)
+        load_wd(1)
+        load_x(0)
+        load_wd(3)
+        load_x(1)
+        nc.sync.dma_start(out=freqs[:], in_=freqs_cis.rearrange("(a p) f c -> p a f c", p=P))
+        load_x(3)
+        load_wk(1)
+        load_wv(3)
+        load_wv(2)
+        load_wv(1)
+        load_x(2)
+
+        ident_f = keep.tile([P, P], F32)
+        ident_b = keep.tile([P, P], BF16)
+        make_identity(nc, ident_b[:])
+        make_identity(nc, ident_f[:])
+        warm = keep.tile([P, 1], F32)
+        nc.vector.memset(warm[:], 0.0)
+        warm2 = keep.tile([P, 1], F32)
+        nc.scalar.activation(out=warm2[:], in_=warm[:], func=COPY)
+        cs = keep.tile([P, T // P, 2, HALF], F32)
+        sc = keep.tile([P, T // P, 2, HALF], F32)
+        nc.gpsimd.tensor_copy(out=cs[:, :, 0, :], in_=freqs[:, :, :, 0])
+        nc.gpsimd.tensor_copy(out=cs[:, :, 1, :], in_=freqs[:, :, :, 1])
+        nc.gpsimd.tensor_scalar(out=sc[:, :, 0, :], in0=freqs[:, :, :, 1], scalar1=-1.0, scalar2=None, op0=MULT)
+        nc.gpsimd.tensor_copy(out=sc[:, :, 1, :], in_=freqs[:, :, :, 0])
+
+        wd_codes = keep.tile([P, PASSES, R], U32, align_bytes=64)
+        wd_scales = keep.tile([P, PASSES, R], U8, align_bytes=64)
+        x_codes = keep.tile([P, TILES, PASSES, P], U32, align_bytes=64)
+        x_scales = keep.tile([P, TILES, PASSES, P], U8, align_bytes=64)
+        kv_codes = keep.tile([P, TILES, P], U32, align_bytes=64)
+        kv_scales = keep.tile([P, TILES, P], U8, align_bytes=64)
+        wk_codes = keep.tile([P, UNITS, UW], U32, align_bytes=64)
+        wk_scales = keep.tile([P, UNITS, UW], U8, align_bytes=64)
+        wv_codes = keep.tile([P, VUNITS, VW], U32, align_bytes=64)
+        wv_scales = keep.tile([P, VUNITS, VW], U8, align_bytes=64)
+
+        def quantize(codes, scales, grouped):
+            nc.vector.quantize_mx(out=codes.bitcast(FP8X4), scales=scales, in_=grouped)
+
+        def mx(out, lhs, rhs, start=True, stop=True):
+            nc.tensor.matmul_mx(out=out, lhsT=lhs[0].bitcast(FP8X4), lhsT_scale=lhs[1], rhs=rhs[0].bitcast(FP8X4), rhs_scale=rhs[1], start=start, stop=stop)
+
+
+        live = {}
+
+        def copy_out(engine, dst, src):
+            if engine == "s":
+                nc.scalar.copy(out=dst, in_=src)
+            else:
+                nc.vector.tensor_copy(out=dst, in_=src)
+
+        def staged(key):
+            if key not in live:
+                grouped = work.tile([P, BANK * PACK], BF16, tag="grouped", align_bytes=64)
+                live[key] = grouped
+            return live[key]
+
+        def wdP(g, h):
+            raw = wd_raw[:, g].rearrange("p j (m t) -> p t m j", t=PACK)
+            bank = psum.tile([P, 2 * BANK], BF16, tag="bank")
+            for s in range(2):
+                nc.tensor.matmul(bank[:, s * BANK : (s + 1) * BANK], lhsT=ident_b[:], rhs=raw[:, 2 * h + s], start=True, stop=True)
+            live["wd", g, h] = bank
+
+        def wdC(g, h, engine):
+            grouped = staged(("wdg", g))
+            copy_out(engine, grouped[:, h * 2 * BANK : (h + 1) * 2 * BANK], live["wd", g, h][:])
+
+        def wdQ(g):
+            quantize(wd_codes[:, g, :], wd_scales[:, g, :], live["wdg", g][:])
+
+        def xP(i, h):
+            words = x_raw[:, i].bitcast(F32)
+            bank = psum.tile([P, 2, 2, P], F32, tag="bank")
+            for s in range(2):
+                g = 2 * h + s
+                for w in range(2):
+                    nc.tensor.transpose(bank[:, s, w, :], words[:, 256 * g + w : 256 * (g + 1) : 2], ident_f[:])
+            live["x", i, h] = bank
+
+        def xC(i, h, engine):
+            grouped = staged(("xg", i))
+            dst = grouped[:, h * 2 * BANK : (h + 1) * 2 * BANK].bitcast(F32)
+            copy_out(engine, dst.rearrange("p (g r w) -> p g r w", g=2, w=2), live["x", i, h][:].rearrange("p g w r -> p g r w"))
+
+        def xQ(i):
+            quantize(x_codes[:, i].rearrange("p g r -> p (g r)"), x_scales[:, i].rearrange("p g r -> p (g r)"), live["xg", i][:])
+
+        def kvP(i):
+            bank = psum.tile([P, PACK, P], F32, tag="bank")
+            for t in range(PACK):
+                cols = slice(t * P, (t + 1) * P)
+                for g in range(PASSES):
+                    mx(bank[:, t, :], (wd_codes[:, g, cols], wd_scales[:, g, cols]), (x_codes[:, i, g, :], x_scales[:, i, g, :]), start=(g == 0), stop=(g == PASSES - 1))
+            live["kv", i] = bank
+
+        def kvC(i, engine):
+            grouped = work.tile([P, P, PACK], BF16, tag="kvg", align_bytes=64)
+            live["kvg", i] = grouped
+            copy_out(engine, grouped[:], live["kv", i][:].rearrange("p t n -> p n t"))
+
+        def kvQ(i):
+            quantize(kv_codes[:, i, :], kv_scales[:, i, :], live["kvg", i][:].rearrange("p n t -> p (n t)"))
+
+        def wn(u, j, engine):
+            wide = (wide0, wide1)[u]
+            src = wk_raw[u][:, j, :].bitcast(FP8)
+            if engine == "s":
+                nc.scalar.activation(out=wide[:, j, :], in_=src, func=COPY, scale=scale[:, j : j + 1])
+            else:
+                nc.vector.tensor_scalar(out=wide[:, j, :], in0=src, scalar1=scale[:, j : j + 1], scalar2=None, op0=MULT)
+
+        PARTS = ((0, 4, DN, 0), (0, 8, DR, DN), (4, 4, DN, 0))
+
+        def il(u, part):
+            wide = (wide0, wide1)[u]
+            first, heads, width, offset = PARTS[part]
+            grouped = staged(("wkg", u, part))
+            src = wide[:].rearrange("p j (h c) -> p h c j", c=DQ)[:, first : first + heads, offset : offset + width, :]
+            nc.vector.tensor_copy(out=grouped[:].rearrange("p (h c j) -> p h c j", h=heads, j=PACK), in_=src)
+
+        def iq(u, part):
+            base = (0, UN, BANK)[part]
+            quantize(wk_codes[:, u, base : base + BANK], wk_scales[:, u, base : base + BANK], live["wkg", u, part][:])
+
+        def kv_lhs(i):
+            return (kv_codes[:, i, :], kv_scales[:, i, :])
+
+        def kout(u, i):
+            if ("ko", u, i) not in live:
+                o = outs.tile([P, UH, DQ], F32, tag="ko", bufs=6, align_bytes=64)
+                live["ko", u, i] = o
+            return live["ko", u, i]
+
+        def kR(u, i):
+            rope = psum.tile([P, UH, 2, HALF], F32, tag="bank")
+            mx(rope[:].rearrange("p h e c -> p (h e c)"), kv_lhs(i), (wk_codes[:, u, UN:UW], wk_scales[:, u, UN:UW]))
+            live["rope", u, i] = rope
+
+        def rope_product(u, i, e, table):
+            full = [P, UH, 2, HALF]
+            a = i % (T // P)
+            prod = outs.tile([P, UH, 2, HALF], F32, name="prod%d" % e, align_bytes=64)
+            nc.vector.tensor_tensor(out=prod[:], in0=live["rope", u, i][:, :, e : e + 1, :].to_broadcast(full), in1=table[:, a : a + 1].to_broadcast(full), op=MULT)
+            live["prod", u, i, e] = prod
+
+        def kA(u, i):
+            rope_product(u, i, 0, cs)
+
+        def kB(u, i):
+            rope_product(u, i, 1, sc)
+
+        def kG(u, i, engine="g"):
+            a, b = (live["prod", u, i, e][:].rearrange("p h e c -> p h (e c)") for e in range(2))
+            o = kout(u, i)
+            if engine == "g":
+                nc.gpsimd.tensor_tensor(out=o[:, :, DN:DQ], in0=a, in1=b, op=ADD)
+            else:
+                nc.vector.tensor_tensor(out=o[:, :, DN:DQ], in0=a, in1=b, op=ADD)
+
+        def kN(u, i, n):
+            cols = slice(n * BANK, (n + 1) * BANK)
+            bank = psum.tile([P, BANK], F32, tag="bank")
+            mx(bank[:], kv_lhs(i), (wk_codes[:, u, cols], wk_scales[:, u, cols]))
+            live["nope", u, i, n] = bank
+
+        def kC(u, i, n, engine):
+            hs = BANK // DN
+            copy_out(engine, kout(u, i)[:, n * hs : (n + 1) * hs, 0:DN], live["nope", u, i, n][:].rearrange("p (h c) -> p h c", c=DN))
+
+        def storeK(u, i, n):
+            hs = UH // 2
+            c0 = u * UW + n * hs * DQ
+            nc.sync.dma_start(out=k_rows[i * P : (i + 1) * P, c0 : c0 + hs * DQ], in_=live["ko", u, i][:, n * hs : (n + 1) * hs, :].rearrange("p h d -> p (h d)"))
+
+        def vI(c, h):
+            grouped = staged(("wvg", c))
+            c0 = (c % 2) * BANK + h * 256
+            src = wv_raw[c // 2][:, :, c0 : c0 + 256]
+            dst = grouped[:, h * 1024 : (h + 1) * 1024]
+            nc.vector.tensor_copy(out=dst.rearrange("p (c i j) -> p c j i", i=4, j=PACK), in_=src.rearrange("p j (c i) -> p c j i", i=4))
+
+        def vP(c, h):
+            bank = psum.tile([P, 2 * BANK], BF16, tag="bank")
+            for s in range(2):
+                c0 = (c % 2) * BANK + h * 256 + s * P
+                src = wv_raw[c // 2][:, :, c0 : c0 + P]
+                nc.tensor.matmul(bank[:, s * BANK : (s + 1) * BANK], lhsT=ident_b[:], rhs=src.rearrange("p j c -> p c j"), start=True, stop=True)
+            live["wv", c, h] = bank
+
+        def vC(c, h, engine):
+            grouped = staged(("wvg", c))
+            copy_out(engine, grouped[:, h * 1024 : (h + 1) * 1024], live["wv", c, h][:])
+
+        def vQ(c):
+            cols = slice((c % 2) * BANK, (c % 2 + 1) * BANK)
+            quantize(wv_codes[:, c // 2, cols], wv_scales[:, c // 2, cols], live["wvg", c][:])
+
+        def vM(c, i):
+            cols = slice((c % 2) * BANK, (c % 2 + 1) * BANK)
+            bank = psum.tile([P, BANK], F32, tag="bank")
+            mx(bank[:], kv_lhs(i), (wv_codes[:, c // 2, cols], wv_scales[:, c // 2, cols]))
+            live["vo", c, i] = bank
+
+        def vX(c, i, engine):
+            o = outs.tile([P, BANK], F32, tag="vo", bufs=8, align_bytes=64)
+            copy_out(engine, o[:], live["vo", c, i][:])
+            live["vs", c, i] = o
+
+        def storeV(c, i):
+            nc.sync.dma_start(out=v_rows[i * P : (i + 1) * P, c * BANK : (c + 1) * BANK], in_=live["vs", c, i][:])
+
+        wide0 = keep.tile([P, PACK, UW], BF16, align_bytes=64)
+        wide1 = keep.tile([P, PACK, UW], BF16, align_bytes=64)
+        ctx.enter_context(tc.manual_schedule())
+        wdP(0, 0)
+        wn(0, 0, "v")
+        wn(0, 1, "s")
+        vI(0, 0)
+        wdP(0, 1)
+        wdP(2, 1)
+        wn(0, 3, "s")
+        vI(0, 1)
+        wdC(0, 1, "s")
+        vQ(0)
+        wn(0, 2, "v")
+        wdP(2, 0)
+        wdP(1, 0)
+        il(0, 2)
+        wdC(0, 0, "s")
+        wdQ(0)
+        wdP(1, 1)
+        xP(0, 0)
+        iq(0, 2)
+        wdC(2, 0, "s")
+        wdC(2, 1, "s")
+        wdC(1, 1, "s")
+        xP(0, 1)
+        wdQ(2)
+        wdP(3, 0)
+        wdP(3, 1)
+        xP(1, 1)
+        xP(1, 0)
+        xC(0, 0, "v")
+        xC(0, 1, "v")
+        wdC(1, 0, "s")
+        wdQ(1)
+        wdC(3, 0, "s")
+        wdC(3, 1, "s")
+        xQ(0)
+        wdQ(3)
+        xC(1, 1, "s")
+        xP(3, 1)
+        il(0, 0)
+        xP(3, 0)
+        xC(1, 0, "s")
+        xQ(1)
+        xC(3, 1, "s")
+        kvP(0)
+        xC(3, 0, "s")
+        iq(0, 0)
+        xQ(3)
+        kvP(1)
+        wn(1, 1, "s")
+        kvC(0, "s")
+        vP(3, 0)
+        vI(3, 1)
+        kvC(1, "s")
+        vC(3, 0, "s")
+        il(0, 1)
+        kvP(3)
+        kvQ(1)
+        vQ(3)
+        kvQ(0)
+        vM(0, 1)
+        iq(0, 1)
+        wn(1, 2, "s")
+        vI(1, 1)
+        kN(0, 0, 1)
+        vM(3, 0)
+        vX(0, 1, "s")
+        vI(1, 0)
+        vX(3, 0, "s")
+        kR(0, 1)
+        kA(0, 1)
+        vM(0, 0)
+        kvC(3, "s")
+        xP(2, 0)
+        kvQ(3)
+        xP(2, 1)
+        vP(2, 1)
+        vQ(1)
+        kB(0, 1)
+        vM(3, 3)
+        vX(0, 0, "s")
+        vX(3, 3, "v")
+        kC(0, 0, 1, "s")
+        vM(1, 0)
+        kR(0, 0)
+        vC(2, 1, "s")
+        xC(2, 0, "s")
+        vX(1, 0, "s")
+        xC(2, 1, "v")
+        kA(0, 0)
+        kN(0, 1, 1)
+        kG(0, 1)
+        vP(2, 0)
+        storeV(0, 1)
+        xQ(2)
+        kN(0, 0, 0)
+        storeV(3, 0)
+        kC(0, 1, 1, "s")
+        kB(0, 0)
+        vC(2, 0, "s")
+        vQ(2)
+        kN(0, 1, 0)
+        kR(0, 3)
+        kG(0, 0)
+        kC(0, 1, 0, "s")
+        storeV(0, 0)
+        vM(1, 3)
+        kvP(2)
+        kA(0, 3)
+        vM(0, 3)
+        vM(2, 0)
+        kN(0, 3, 0)
+        kC(0, 0, 0, "s")
+        kvC(2, "v")
+        kB(0, 3)
+        storeV(3, 3)
+        wn(1, 3, "s")
+        kvQ(2)
+        wn(1, 0, "s")
+        kR(0, 2)
+        storeV(1, 0)
+        vX(0, 3, "v")
+        vM(3, 2)
+        storeK(0, 1, 1)
+        vX(1, 3, "v")
+        storeK(0, 1, 0)
+        vX(2, 0, "s")
+        kG(0, 3)
+        storeK(0, 0, 1)
+        vX(3, 2, "s")
+        vM(2, 2)
+        vM(0, 2)
+        kA(0, 2)
+        il(1, 1)
+        kC(0, 3, 0, "s")
+        vM(2, 1)
+        vM(1, 2)
+        storeK(0, 0, 0)
+        storeV(0, 3)
+        il(1, 0)
+        storeV(1, 3)
+        vX(2, 1, "s")
+        vM(2, 3)
+        vM(1, 1)
+        storeV(2, 0)
+        vX(0, 2, "s")
+        storeV(3, 2)
+        vX(2, 3, "s")
+        kB(0, 2)
+        vX(1, 2, "s")
+        vX(1, 1, "s")
+        iq(1, 1)
+        vM(3, 1)
+        vX(2, 2, "s")
+        storeK(0, 3, 0)
+        iq(1, 0)
+        storeV(2, 1)
+        il(1, 2)
+        kR(1, 3)
+        kN(0, 3, 1)
+        storeV(0, 2)
+        kA(1, 3)
+        kN(0, 2, 0)
+        kG(0, 2)
+        storeV(2, 3)
+        kN(1, 3, 0)
+        storeV(1, 2)
+        kN(0, 2, 1)
+        kB(1, 3)
+        vX(3, 1, "s")
+        kN(1, 2, 0)
+        iq(1, 2)
+        storeV(1, 1)
+        kN(1, 0, 0)
+        kR(1, 0)
+        kC(0, 3, 1, "s")
+        kC(0, 2, 1, "s")
+        kR(1, 2)
+        kG(1, 3)
+        kN(1, 3, 1)
+        kC(1, 3, 0, "s")
+        kA(1, 0)
+        kC(0, 2, 0, "s")
+        storeV(3, 1)
+        kN(1, 1, 0)
+        kB(1, 0)
+        storeV(2, 2)
+        storeK(0, 3, 1)
+        storeK(0, 2, 1)
+        kG(1, 0)
+        kR(1, 1)
+        kA(1, 1)
+        kN(1, 0, 1)
+        storeK(0, 2, 0)
+        kB(1, 1)
+        kG(1, 1)
+        kC(1, 3, 1, "s")
+        kC(1, 0, 0, "v")
+        kC(1, 2, 0, "s")
+        kA(1, 2)
+        storeK(1, 3, 1)
+        storeK(1, 3, 0)
+        kN(1, 2, 1)
+        kC(1, 0, 1, "s")
+        kC(1, 2, 1, "v")
+        kC(1, 1, 0, "s")
+        storeK(1, 0, 1)
+        kN(1, 1, 1)
+        kB(1, 2)
+        kC(1, 1, 1, "s")
+        kG(1, 2)
+        storeK(1, 0, 0)
+        storeK(1, 1, 0)
+        storeK(1, 1, 1)
+        storeK(1, 2, 1)
+        storeK(1, 2, 0)

@@ -54,8 +54,8 @@ def tile_fa3mlaattention_pa_kernel(tc, x, freqs_cis, w_kv_down, w_k_up_bytes, w_
         for u in range(UNITS):
             raw_k = keep.tile([P, PACK, UW], U8, name="wk_raw%d" % u, align_bytes=64)
             wk_raw.append(raw_k)
-        for u in range(VUNITS):
-            raw_v = keep.tile([P, PACK, VW], BF16, name="wv_raw%d" % u, align_bytes=64)
+        for c in range(H * DV // BANK):
+            raw_v = keep.tile([P, PACK, BANK], BF16, name="wv_raw%d" % c, align_bytes=64)
             wv_raw.append(raw_v)
         wd_view = w_kv_down.rearrange("(g p j) n -> g p j n", p=P, j=PACK)
         wk_view = w_k_up_bytes.rearrange("(p j) n -> p j n", j=PACK)
@@ -75,27 +75,27 @@ def tile_fa3mlaattention_pa_kernel(tc, x, freqs_cis, w_kv_down, w_k_up_bytes, w_
 
         def load_wv(c):
             cols = slice(c * BANK, (c + 1) * BANK)
-            nc.sync.dma_start(out=wv_raw[c // 2][:, :, (c % 2) * BANK : (c % 2 + 1) * BANK], in_=wv_view[:, :, cols])
+            nc.sync.dma_start(out=wv_raw[c][:], in_=wv_view[:, :, cols])
 
-        load_wka(0)
-        load_wka(1)
+        load_wka(2)
         nc.sync.dma_start(out=scale[:], in_=w_k_up_scale.rearrange("(p j) o -> p (j o)", j=PACK))
+        load_wka(0)
         load_wv(0)
         load_wka(3)
-        load_wd(0)
-        load_wka(2)
-        load_wd(2)
+        load_wka(1)
         load_wd(1)
-        load_x(0)
+        load_wd(0)
+        load_wd(2)
         load_wd(3)
+        load_x(0)
         load_x(1)
-        nc.sync.dma_start(out=freqs[:], in_=freqs_cis.rearrange("(a p) f c -> p a f c", p=P))
+        load_x(2)
         load_x(3)
         load_wk(1)
-        load_wv(3)
-        load_wv(2)
+        nc.sync.dma_start(out=freqs[:], in_=freqs_cis.rearrange("(a p) f c -> p a f c", p=P))
         load_wv(1)
-        load_x(2)
+        load_wv(2)
+        load_wv(3)
 
         ident_f = keep.tile([P, P], F32)
         ident_b = keep.tile([P, P], BF16)
@@ -264,16 +264,16 @@ def tile_fa3mlaattention_pa_kernel(tc, x, freqs_cis, w_kv_down, w_k_up_bytes, w_
 
         def vI(c, h):
             grouped = staged(("wvg", c))
-            c0 = (c % 2) * BANK + h * 256
-            src = wv_raw[c // 2][:, :, c0 : c0 + 256]
+            c0 = h * 256
+            src = wv_raw[c][:, :, c0 : c0 + 256]
             dst = grouped[:, h * 1024 : (h + 1) * 1024]
             nc.vector.tensor_copy(out=dst.rearrange("p (c i j) -> p c j i", i=4, j=PACK), in_=src.rearrange("p j (c i) -> p c j i", i=4))
 
         def vP(c, h):
             bank = psum.tile([P, 2 * BANK], BF16, tag="bank")
             for s in range(2):
-                c0 = (c % 2) * BANK + h * 256 + s * P
-                src = wv_raw[c // 2][:, :, c0 : c0 + P]
+                c0 = h * 256 + s * P
+                src = wv_raw[c][:, :, c0 : c0 + P]
                 nc.tensor.matmul(bank[:, s * BANK : (s + 1) * BANK], lhsT=ident_b[:], rhs=src.rearrange("p j c -> p c j"), start=True, stop=True)
             live["wv", c, h] = bank
 
@@ -302,218 +302,218 @@ def tile_fa3mlaattention_pa_kernel(tc, x, freqs_cis, w_kv_down, w_k_up_bytes, w_
         wide0 = keep.tile([P, PACK, UW], BF16, align_bytes=64)
         wide1 = keep.tile([P, PACK, UW], BF16, align_bytes=64)
         ctx.enter_context(tc.manual_schedule())
-        wdP(0, 0)
-        wn(0, 0, "v")
-        wn(0, 1, "s")
-        vI(0, 0)
-        wdP(0, 1)
-        wdP(2, 1)
-        wn(0, 3, "s")
-        vI(0, 1)
-        wdC(0, 1, "s")
-        vQ(0)
-        wn(0, 2, "v")
-        wdP(2, 0)
-        wdP(1, 0)
-        il(0, 2)
-        wdC(0, 0, "s")
-        wdQ(0)
         wdP(1, 1)
-        xP(0, 0)
-        iq(0, 2)
-        wdC(2, 0, "s")
-        wdC(2, 1, "s")
+        wn(0, 2, "s")
+        wdP(1, 0)
+        wn(0, 3, "s")
+        wdP(0, 1)
+        wn(0, 0, "v")
+        vI(0, 0)
+        wdP(0, 0)
         wdC(1, 1, "s")
+        vI(0, 1)
+        wn(0, 1, "v")
+        wdP(2, 0)
+        vQ(0)
+        wdP(2, 1)
+        wdC(1, 0, "s")
+        wdP(3, 0)
+        il(0, 2)
+        wdC(0, 1, "s")
+        wdP(3, 1)
+        wdQ(1)
+        iq(0, 2)
+        wdC(0, 0, "s")
+        wdC(2, 0, "s")
+        xP(0, 0)
+        wdC(2, 1, "s")
+        wdC(3, 1, "s")
+        wdQ(0)
         xP(0, 1)
         wdQ(2)
-        wdP(3, 0)
-        wdP(3, 1)
-        xP(1, 1)
         xP(1, 0)
-        xC(0, 0, "v")
-        xC(0, 1, "v")
-        wdC(1, 0, "s")
-        wdQ(1)
         wdC(3, 0, "s")
-        wdC(3, 1, "s")
-        xQ(0)
-        wdQ(3)
-        xC(1, 1, "s")
-        xP(3, 1)
+        xP(1, 1)
         il(0, 0)
-        xP(3, 0)
-        xC(1, 0, "s")
-        xQ(1)
-        xC(3, 1, "s")
-        kvP(0)
-        xC(3, 0, "s")
+        wdQ(3)
+        xC(0, 0, "s")
         iq(0, 0)
+        xP(2, 1)
+        xC(0, 1, "s")
+        xP(2, 0)
+        xP(3, 0)
+        xP(3, 1)
+        xC(1, 0, "s")
+        xQ(0)
+        xC(1, 1, "s")
+        xC(2, 1, "s")
+        kvP(0)
+        xC(2, 0, "v")
+        xQ(1)
+        xC(3, 0, "s")
+        xC(3, 1, "s")
+        xQ(2)
         xQ(3)
         kvP(1)
-        wn(1, 1, "s")
-        kvC(0, "s")
-        vP(3, 0)
-        vI(3, 1)
-        kvC(1, "s")
-        vC(3, 0, "s")
-        il(0, 1)
         kvP(3)
-        kvQ(1)
-        vQ(3)
-        kvQ(0)
-        vM(0, 1)
-        iq(0, 1)
-        wn(1, 2, "s")
+        vP(2, 1)
+        il(0, 1)
         vI(1, 1)
-        kN(0, 0, 1)
-        vM(3, 0)
-        vX(0, 1, "s")
+        wn(1, 0, "s")
+        kvC(0, "s")
+        kvC(1, "s")
         vI(1, 0)
-        vX(3, 0, "s")
+        kvQ(1)
+        wn(1, 1, "s")
+        iq(0, 1)
+        vI(3, 1)
+        kvC(3, "s")
+        vP(3, 0)
+        kvQ(0)
         kR(0, 1)
         kA(0, 1)
-        vM(0, 0)
-        kvC(3, "s")
-        xP(2, 0)
         kvQ(3)
-        xP(2, 1)
-        vP(2, 1)
+        kN(0, 1, 0)
         vQ(1)
-        kB(0, 1)
-        vM(3, 3)
+        vC(2, 1, "s")
+        kvP(2)
+        vC(3, 0, "s")
+        kC(0, 1, 0, "s")
+        vM(0, 3)
+        vQ(3)
+        vM(0, 0)
+        vX(0, 3, "s")
+        vM(1, 3)
         vX(0, 0, "s")
-        vX(3, 3, "v")
-        kC(0, 0, 1, "s")
         vM(1, 0)
         kR(0, 0)
-        vC(2, 1, "s")
-        xC(2, 0, "s")
-        vX(1, 0, "s")
-        xC(2, 1, "v")
+        kB(0, 1)
+        kR(0, 3)
+        vX(1, 3, "v")
         kA(0, 0)
+        kvC(2, "s")
+        kA(0, 3)
+        vP(2, 0)
+        vM(3, 3)
+        storeV(0, 3)
+        vX(1, 0, "s")
+        storeV(0, 0)
+        vC(2, 0, "s")
         kN(0, 1, 1)
         kG(0, 1)
-        vP(2, 0)
-        storeV(0, 1)
-        xQ(2)
-        kN(0, 0, 0)
-        storeV(3, 0)
-        kC(0, 1, 1, "s")
+        vM(3, 0)
         kB(0, 0)
-        vC(2, 0, "s")
-        vQ(2)
-        kN(0, 1, 0)
-        kR(0, 3)
-        kG(0, 0)
-        kC(0, 1, 0, "s")
-        storeV(0, 0)
-        vM(1, 3)
-        kvP(2)
-        kA(0, 3)
-        vM(0, 3)
-        vM(2, 0)
-        kN(0, 3, 0)
-        kC(0, 0, 0, "s")
-        kvC(2, "v")
-        kB(0, 3)
-        storeV(3, 3)
-        wn(1, 3, "s")
         kvQ(2)
-        wn(1, 0, "s")
-        kR(0, 2)
-        storeV(1, 0)
-        vX(0, 3, "v")
-        vM(3, 2)
-        storeK(0, 1, 1)
-        vX(1, 3, "v")
-        storeK(0, 1, 0)
-        vX(2, 0, "s")
-        kG(0, 3)
-        storeK(0, 0, 1)
-        vX(3, 2, "s")
-        vM(2, 2)
-        vM(0, 2)
-        kA(0, 2)
-        il(1, 1)
-        kC(0, 3, 0, "s")
-        vM(2, 1)
-        vM(1, 2)
-        storeK(0, 0, 0)
-        storeV(0, 3)
-        il(1, 0)
+        kN(0, 0, 0)
+        kN(0, 0, 1)
         storeV(1, 3)
-        vX(2, 1, "s")
-        vM(2, 3)
+        vX(3, 3, "s")
+        wn(1, 3, "s")
+        vM(0, 1)
+        kC(0, 1, 1, "v")
+        kG(0, 0)
+        kB(0, 3)
         vM(1, 1)
-        storeV(2, 0)
-        vX(0, 2, "s")
-        storeV(3, 2)
-        vX(2, 3, "s")
+        vX(0, 1, "v")
+        kR(0, 2)
+        kG(0, 3)
+        kN(0, 3, 0)
+        vX(3, 0, "v")
+        kC(0, 0, 0, "s")
+        vM(3, 2)
+        vM(0, 2)
+        vX(1, 1, "v")
+        wn(1, 2, "s")
+        storeV(1, 0)
+        kA(0, 2)
+        vQ(2)
         kB(0, 2)
-        vX(1, 2, "s")
-        vX(1, 1, "s")
-        iq(1, 1)
+        kC(0, 0, 1, "s")
+        il(1, 1)
+        vM(2, 0)
+        vX(2, 0, "s")
+        vM(1, 2)
+        kC(0, 3, 0, "s")
+        storeK(0, 1, 0)
+        storeV(3, 3)
+        storeK(0, 1, 1)
+        vM(2, 1)
         vM(3, 1)
-        vX(2, 2, "s")
-        storeK(0, 3, 0)
-        iq(1, 0)
-        storeV(2, 1)
         il(1, 2)
-        kR(1, 3)
+        iq(1, 1)
+        storeV(0, 1)
+        vX(1, 2, "s")
+        storeV(3, 0)
+        vX(0, 2, "s")
+        storeV(1, 1)
+        vM(2, 2)
         kN(0, 3, 1)
-        storeV(0, 2)
+        iq(1, 2)
+        vX(3, 2, "s")
+        storeK(0, 0, 0)
+        vM(2, 3)
+        kR(1, 3)
+        vX(2, 2, "s")
+        kN(1, 1, 1)
+        storeK(0, 0, 1)
         kA(1, 3)
+        storeV(2, 0)
+        kN(1, 3, 1)
+        vX(2, 1, "s")
+        kB(1, 3)
         kN(0, 2, 0)
         kG(0, 2)
-        storeV(2, 3)
-        kN(1, 3, 0)
-        storeV(1, 2)
-        kN(0, 2, 1)
-        kB(1, 3)
         vX(3, 1, "s")
-        kN(1, 2, 0)
-        iq(1, 2)
-        storeV(1, 1)
-        kN(1, 0, 0)
-        kR(1, 0)
+        il(1, 0)
+        kN(0, 2, 1)
         kC(0, 3, 1, "s")
+        vX(2, 3, "s")
         kC(0, 2, 1, "s")
-        kR(1, 2)
-        kG(1, 3)
-        kN(1, 3, 1)
-        kC(1, 3, 0, "s")
-        kA(1, 0)
+        kN(1, 0, 1)
+        kC(1, 3, 1, "s")
+        kC(1, 1, 1, "s")
+        storeK(0, 3, 0)
+        storeV(1, 2)
+        kR(1, 0)
+        iq(1, 0)
+        kN(1, 2, 1)
         kC(0, 2, 0, "s")
+        kN(1, 0, 0)
+        storeV(3, 2)
+        kA(1, 0)
+        storeV(0, 2)
+        storeV(2, 1)
         storeV(3, 1)
-        kN(1, 1, 0)
-        kB(1, 0)
+        kN(1, 3, 0)
+        kC(1, 0, 1, "v")
+        kR(1, 1)
         storeV(2, 2)
+        kB(1, 0)
+        kA(1, 1)
+        kG(1, 3)
         storeK(0, 3, 1)
+        kC(1, 3, 0, "s")
+        kN(1, 1, 0)
+        storeV(2, 3)
         storeK(0, 2, 1)
         kG(1, 0)
-        kR(1, 1)
-        kA(1, 1)
-        kN(1, 0, 1)
+        kN(1, 2, 0)
         storeK(0, 2, 0)
-        kB(1, 1)
-        kG(1, 1)
-        kC(1, 3, 1, "s")
-        kC(1, 0, 0, "v")
-        kC(1, 2, 0, "s")
-        kA(1, 2)
         storeK(1, 3, 1)
+        kC(1, 1, 0, "v")
+        kC(1, 2, 0, "s")
         storeK(1, 3, 0)
-        kN(1, 2, 1)
-        kC(1, 0, 1, "s")
-        kC(1, 2, 1, "v")
-        kC(1, 1, 0, "s")
+        kC(1, 0, 0, "s")
+        kB(1, 1)
         storeK(1, 0, 1)
-        kN(1, 1, 1)
-        kB(1, 2)
-        kC(1, 1, 1, "s")
-        kG(1, 2)
+        kR(1, 2)
+        kA(1, 2)
+        kG(1, 1)
         storeK(1, 0, 0)
+        kC(1, 2, 1, "v")
         storeK(1, 1, 0)
         storeK(1, 1, 1)
+        kB(1, 2)
+        kG(1, 2)
         storeK(1, 2, 1)
         storeK(1, 2, 0)

@@ -77,23 +77,23 @@ def tile_fa3mlaattention_pa_kernel(tc, x, freqs_cis, w_kv_down, w_k_up_bytes, w_
             cols = slice(c * BANK, (c + 1) * BANK)
             nc.sync.dma_start(out=wv_raw[c][:], in_=wv_view[:, :, cols])
 
-        load_wka(2)
-        nc.sync.dma_start(out=scale[:], in_=w_k_up_scale.rearrange("(p j) o -> p (j o)", j=PACK))
-        load_wka(0)
-        load_wv(0)
-        load_wka(3)
-        load_wka(1)
         load_wd(1)
+        load_wv(0)
         load_wd(0)
-        load_wd(2)
-        load_wd(3)
+        load_wka(0)
+        load_wka(3)
+        nc.sync.dma_start(out=scale[:], in_=w_k_up_scale.rearrange("(p j) o -> p (j o)", j=PACK))
         load_x(0)
+        load_wd(2)
+        load_wka(1)
+        load_wka(2)
         load_x(1)
-        load_x(2)
+        load_wd(3)
         load_x(3)
         load_wk(1)
-        nc.sync.dma_start(out=freqs[:], in_=freqs_cis.rearrange("(a p) f c -> p a f c", p=P))
+        load_x(2)
         load_wv(1)
+        nc.sync.dma_start(out=freqs[:], in_=freqs_cis.rearrange("(a p) f c -> p a f c", p=P))
         load_wv(2)
         load_wv(3)
 
@@ -145,10 +145,11 @@ def tile_fa3mlaattention_pa_kernel(tc, x, freqs_cis, w_kv_down, w_k_up_bytes, w_
             return live[key]
 
         def wdP(g, h):
-            raw = wd_raw[:, g].rearrange("p j (m t) -> p t m j", t=PACK)
+            raw = wd_raw[:, g].rearrange("p j (m t) -> p j m t", t=PACK)
             bank = psum.tile([P, 2 * BANK], BF16, tag="bank")
-            for s in range(2):
-                nc.tensor.matmul(bank[:, s * BANK : (s + 1) * BANK], lhsT=ident_b[:], rhs=raw[:, 2 * h + s], start=True, stop=True)
+            dst = bank[:].rearrange("p (t m j) -> p j m t", t=2, j=PACK)
+            for j in range(0, PACK, 2):
+                nc.tensor.matmul(dst[:, j : j + 2], lhsT=ident_b[:], rhs=raw[:, j : j + 2, :, 2 * h : 2 * h + 2], start=True, stop=True)
             live["wd", g, h] = bank
 
         def wdC(g, h, engine):
@@ -206,7 +207,13 @@ def tile_fa3mlaattention_pa_kernel(tc, x, freqs_cis, w_kv_down, w_k_up_bytes, w_
             first, heads, width, offset = PARTS[part]
             grouped = staged(("wkg", u, part))
             src = wide[:].rearrange("p j (h c) -> p h c j", c=DQ)[:, first : first + heads, offset : offset + width, :]
-            nc.vector.tensor_copy(out=grouped[:].rearrange("p (h c j) -> p h c j", h=heads, j=PACK), in_=src)
+            if part == 1:
+                nc.vector.tensor_copy(out=grouped[:].rearrange("p (h c j) -> p h c j", h=heads, j=PACK), in_=src)
+            else:
+                nc.vector.tensor_copy(
+                    out=grouped[:].rearrange("p (h c i j) -> p h c j i", h=heads, i=4, j=PACK),
+                    in_=src.rearrange("p h (c i) j -> p h c j i", i=4),
+                )
 
         def iq(u, part):
             base = (0, UN, BANK)[part]
@@ -271,10 +278,9 @@ def tile_fa3mlaattention_pa_kernel(tc, x, freqs_cis, w_kv_down, w_k_up_bytes, w_
 
         def vP(c, h):
             bank = psum.tile([P, 2 * BANK], BF16, tag="bank")
-            for s in range(2):
-                c0 = h * 256 + s * P
-                src = wv_raw[c][:, :, c0 : c0 + P]
-                nc.tensor.matmul(bank[:, s * BANK : (s + 1) * BANK], lhsT=ident_b[:], rhs=src.rearrange("p j c -> p c j"), start=True, stop=True)
+            dst = bank[:].rearrange("p (c j) -> p j c", j=PACK)
+            for j in range(0, PACK, 2):
+                nc.tensor.matmul(dst[:, j : j + 2], lhsT=ident_b[:], rhs=wv_raw[c][:, j : j + 2, h * 256 : (h + 1) * 256], start=True, stop=True)
             live["wv", c, h] = bank
 
         def vC(c, h, engine):
@@ -302,218 +308,218 @@ def tile_fa3mlaattention_pa_kernel(tc, x, freqs_cis, w_kv_down, w_k_up_bytes, w_
         wide0 = keep.tile([P, PACK, UW], BF16, align_bytes=64)
         wide1 = keep.tile([P, PACK, UW], BF16, align_bytes=64)
         ctx.enter_context(tc.manual_schedule())
-        wdP(1, 1)
-        wn(0, 2, "s")
         wdP(1, 0)
-        wn(0, 3, "s")
-        wdP(0, 1)
-        wn(0, 0, "v")
-        vI(0, 0)
-        wdP(0, 0)
+        wdP(1, 1)
         wdC(1, 1, "s")
+        wdC(1, 0, "v")
+        vI(0, 0)
         vI(0, 1)
-        wn(0, 1, "v")
-        wdP(2, 0)
+        wdP(0, 1)
+        wn(0, 3, "v")
+        wdP(0, 0)
+        xP(0, 1)
+        xP(0, 0)
+        wdC(0, 1, "s")
         vQ(0)
         wdP(2, 1)
-        wdC(1, 0, "s")
-        wdP(3, 0)
-        il(0, 2)
-        wdC(0, 1, "s")
-        wdP(3, 1)
-        wdQ(1)
-        iq(0, 2)
-        wdC(0, 0, "s")
-        wdC(2, 0, "s")
-        xP(0, 0)
-        wdC(2, 1, "s")
-        wdC(3, 1, "s")
-        wdQ(0)
-        xP(0, 1)
-        wdQ(2)
-        xP(1, 0)
-        wdC(3, 0, "s")
+        wdP(2, 0)
         xP(1, 1)
-        il(0, 0)
-        wdQ(3)
+        wdC(0, 0, "v")
+        wn(0, 0, "s")
+        wn(0, 1, "s")
+        wdQ(1)
+        xP(1, 0)
         xC(0, 0, "s")
-        iq(0, 0)
-        xP(2, 1)
         xC(0, 1, "s")
-        xP(2, 0)
-        xP(3, 0)
-        xP(3, 1)
-        xC(1, 0, "s")
-        xQ(0)
+        wdQ(0)
         xC(1, 1, "s")
-        xC(2, 1, "s")
-        kvP(0)
-        xC(2, 0, "v")
+        wn(0, 2, "v")
+        il(0, 2)
+        xQ(0)
+        xC(1, 0, "s")
+        wdC(2, 0, "s")
+        iq(0, 2)
+        wdP(3, 0)
+        wdC(2, 1, "s")
         xQ(1)
-        xC(3, 0, "s")
+        wdP(3, 1)
+        xP(3, 0)
+        wdC(3, 0, "s")
+        wdC(3, 1, "s")
+        wn(1, 3, "s")
+        il(0, 0)
+        wdQ(2)
+        xP(3, 1)
         xC(3, 1, "s")
-        xQ(2)
-        xQ(3)
-        kvP(1)
-        kvP(3)
-        vP(2, 1)
+        wdQ(3)
+        xP(2, 1)
+        iq(0, 0)
         il(0, 1)
-        vI(1, 1)
-        wn(1, 0, "s")
-        kvC(0, "s")
+        kvP(1)
+        kvP(0)
+        xC(3, 0, "s")
         kvC(1, "s")
-        vI(1, 0)
+        xQ(3)
+        kvP(3)
+        iq(0, 1)
+        xC(2, 1, "s")
         kvQ(1)
         wn(1, 1, "s")
-        iq(0, 1)
-        vI(3, 1)
         kvC(3, "s")
-        vP(3, 0)
+        vM(0, 1)
+        vI(1, 0)
+        xP(2, 0)
+        kN(0, 1, 0)
+        kN(0, 1, 1)
+        kvC(0, "s")
+        wn(1, 2, "v")
+        vI(1, 1)
+        kvQ(3)
+        vI(3, 1)
+        vM(0, 3)
+        vX(0, 1, "s")
         kvQ(0)
         kR(0, 1)
-        kA(0, 1)
-        kvQ(3)
-        kN(0, 1, 0)
-        vQ(1)
-        vC(2, 1, "s")
-        kvP(2)
-        vC(3, 0, "s")
-        kC(0, 1, 0, "s")
-        vM(0, 3)
-        vQ(3)
-        vM(0, 0)
         vX(0, 3, "s")
-        vM(1, 3)
-        vX(0, 0, "s")
+        vQ(1)
+        xC(2, 0, "s")
+        vM(0, 0)
+        storeV(0, 1)
+        vP(3, 0)
+        kA(0, 1)
+        kC(0, 1, 0, "s")
         vM(1, 0)
+        vX(0, 0, "v")
+        kC(0, 1, 1, "s")
         kR(0, 0)
-        kB(0, 1)
-        kR(0, 3)
-        vX(1, 3, "v")
-        kA(0, 0)
-        kvC(2, "s")
-        kA(0, 3)
-        vP(2, 0)
-        vM(3, 3)
         storeV(0, 3)
-        vX(1, 0, "s")
-        storeV(0, 0)
-        vC(2, 0, "s")
-        kN(0, 1, 1)
-        kG(0, 1)
-        vM(3, 0)
-        kB(0, 0)
-        kvQ(2)
-        kN(0, 0, 0)
-        kN(0, 0, 1)
-        storeV(1, 3)
-        vX(3, 3, "s")
-        wn(1, 3, "s")
-        vM(0, 1)
-        kC(0, 1, 1, "v")
-        kG(0, 0)
-        kB(0, 3)
+        kB(0, 1)
         vM(1, 1)
-        vX(0, 1, "v")
-        kR(0, 2)
-        kG(0, 3)
-        kN(0, 3, 0)
-        vX(3, 0, "v")
-        kC(0, 0, 0, "s")
-        vM(3, 2)
-        vM(0, 2)
-        vX(1, 1, "v")
-        wn(1, 2, "s")
+        kA(0, 0)
+        vX(1, 0, "s")
+        vM(1, 3)
+        vX(1, 1, "s")
+        vX(1, 3, "v")
+        kG(0, 1)
+        kB(0, 0)
+        kN(0, 0, 1)
+        vP(2, 1)
+        kR(0, 3)
+        vC(3, 0, "s")
+        vQ(3)
+        storeV(0, 0)
         storeV(1, 0)
-        kA(0, 2)
-        vQ(2)
-        kB(0, 2)
+        xQ(2)
+        storeV(1, 1)
+        kA(0, 3)
+        storeV(1, 3)
+        kN(0, 0, 0)
+        vC(2, 1, "v")
         kC(0, 0, 1, "s")
-        il(1, 1)
+        kG(0, 0)
+        vP(2, 0)
+        storeK(0, 1, 0)
+        vM(3, 0)
+        storeK(0, 1, 1)
+        wn(1, 0, "s")
+        vC(2, 0, "s")
+        kB(0, 3)
+        vQ(2)
+        storeK(0, 0, 1)
+        kvP(2)
+        vM(3, 3)
+        il(1, 2)
+        kC(0, 0, 0, "s")
+        vX(3, 0, "s")
+        kvC(2, "s")
+        vX(3, 3, "s")
+        vM(3, 1)
+        vX(3, 1, "s")
+        vM(2, 1)
+        kvQ(2)
+        storeK(0, 0, 0)
         vM(2, 0)
+        kR(0, 2)
+        vX(2, 1, "s")
+        il(1, 1)
         vX(2, 0, "s")
         vM(1, 2)
-        kC(0, 3, 0, "s")
-        storeK(0, 1, 0)
-        storeV(3, 3)
-        storeK(0, 1, 1)
-        vM(2, 1)
-        vM(3, 1)
-        il(1, 2)
-        iq(1, 1)
-        storeV(0, 1)
-        vX(1, 2, "s")
+        vM(3, 2)
+        vM(0, 2)
         storeV(3, 0)
-        vX(0, 2, "s")
-        storeV(1, 1)
-        vM(2, 2)
+        storeV(3, 3)
+        vX(1, 2, "s")
         kN(0, 3, 1)
-        iq(1, 2)
-        vX(3, 2, "s")
-        storeK(0, 0, 0)
-        vM(2, 3)
-        kR(1, 3)
+        kA(0, 2)
+        kG(0, 3)
+        vM(2, 2)
+        kN(0, 3, 0)
         vX(2, 2, "s")
-        kN(1, 1, 1)
-        storeK(0, 0, 1)
-        kA(1, 3)
-        storeV(2, 0)
-        kN(1, 3, 1)
-        vX(2, 1, "s")
-        kB(1, 3)
-        kN(0, 2, 0)
-        kG(0, 2)
-        vX(3, 1, "s")
-        il(1, 0)
-        kN(0, 2, 1)
+        vM(2, 3)
+        vX(0, 2, "s")
+        kB(0, 2)
         kC(0, 3, 1, "s")
+        kN(0, 2, 0)
+        storeV(3, 1)
+        kC(0, 3, 0, "s")
+        kC(0, 2, 0, "s")
+        iq(1, 1)
+        vX(3, 2, "s")
+        storeV(2, 1)
+        iq(1, 2)
+        storeV(2, 0)
+        kR(1, 2)
+        kN(0, 2, 1)
+        il(1, 0)
+        storeV(1, 2)
         vX(2, 3, "s")
+        kA(1, 2)
+        storeV(2, 2)
+        storeV(0, 2)
+        kN(1, 2, 1)
+        kN(1, 1, 1)
+        kR(1, 1)
+        kC(1, 2, 1, "s")
+        kG(0, 2)
+        kB(1, 2)
+        iq(1, 0)
+        storeK(0, 3, 1)
         kC(0, 2, 1, "s")
-        kN(1, 0, 1)
-        kC(1, 3, 1, "s")
+        kR(1, 3)
         kC(1, 1, 1, "s")
         storeK(0, 3, 0)
-        storeV(1, 2)
-        kR(1, 0)
-        iq(1, 0)
-        kN(1, 2, 1)
-        kC(0, 2, 0, "s")
-        kN(1, 0, 0)
         storeV(3, 2)
-        kA(1, 0)
-        storeV(0, 2)
-        storeV(2, 1)
-        storeV(3, 1)
-        kN(1, 3, 0)
-        kC(1, 0, 1, "v")
-        kR(1, 1)
-        storeV(2, 2)
-        kB(1, 0)
         kA(1, 1)
-        kG(1, 3)
-        storeK(0, 3, 1)
+        kN(1, 3, 1)
+        kB(1, 1)
+        kA(1, 3)
+        kC(1, 3, 1, "s")
+        kN(1, 2, 0)
+        kG(1, 2)
+        storeV(2, 3)
+        kR(1, 0)
+        kG(1, 1)
+        kC(1, 2, 0, "s")
+        kN(1, 0, 0)
+        kN(1, 3, 0)
+        storeK(0, 2, 0)
+        kB(1, 3)
+        kN(1, 0, 1)
+        storeK(0, 2, 1)
         kC(1, 3, 0, "s")
         kN(1, 1, 0)
-        storeV(2, 3)
-        storeK(0, 2, 1)
-        kG(1, 0)
-        kN(1, 2, 0)
-        storeK(0, 2, 0)
-        storeK(1, 3, 1)
-        kC(1, 1, 0, "v")
-        kC(1, 2, 0, "s")
-        storeK(1, 3, 0)
-        kC(1, 0, 0, "s")
-        kB(1, 1)
-        storeK(1, 0, 1)
-        kR(1, 2)
-        kA(1, 2)
-        kG(1, 1)
-        storeK(1, 0, 0)
-        kC(1, 2, 1, "v")
-        storeK(1, 1, 0)
-        storeK(1, 1, 1)
-        kB(1, 2)
-        kG(1, 2)
         storeK(1, 2, 1)
+        kC(1, 0, 0, "v")
         storeK(1, 2, 0)
+        kA(1, 0)
+        storeK(1, 1, 1)
+        kC(1, 1, 0, "s")
+        storeK(1, 1, 0)
+        kB(1, 0)
+        kG(1, 3)
+        storeK(1, 3, 1)
+        kC(1, 0, 1, "s")
+        kG(1, 0)
+        storeK(1, 3, 0)
+        storeK(1, 0, 0)
+        storeK(1, 0, 1)

from contextlib import ExitStack

import concourse.mybir as mybir
from concourse.masks import make_identity

F32 = mybir.dt.float32
BF16 = mybir.dt.bfloat16
U32 = mybir.dt.uint32
U8 = mybir.dt.uint8
FP8 = mybir.dt.float8_e4m3fn
FP8X4 = mybir.dt.float8_e4m3fn_x4
MULT = mybir.AluOpType.mult
ADD = mybir.AluOpType.add
COPY = mybir.ActivationFunctionType.Copy

B, T, C, R, H, DN, DR, DV = 2, 256, 2048, 512, 16, 128, 64, 128
DQ = DN + DR
HALF = DR // 2
P = 128
PACK = 4
KP = P * PACK
PASSES = C // KP
TILES = B * T // P
BANK = 512
UH = 8
UNITS = H // UH
UW = UH * DQ
UN = UH * DN
UR = UH * DR
VW = 1024
VUNITS = H * DV // VW

FLOPS = 2 * B * T * C * R + 2 * B * T * R * H * (DQ + DV)


def tile_fa3mlaattention_pa_kernel(tc, x, freqs_cis, w_kv_down, w_k_up_bytes, w_k_up_scale, w_v_up, out_0, out_1):
    nc = tc.nc
    x_rows = x.rearrange("b t c -> (b t) c")
    k_rows = out_0.rearrange("b t h d -> (b t) (h d)")
    v_rows = out_1.rearrange("b t h d -> (b t) (h d)")

    with ExitStack() as ctx:
        keep = ctx.enter_context(tc.tile_pool(name="keep", bufs=1))
        work = ctx.enter_context(tc.tile_pool(name="work", bufs=3))
        outs = ctx.enter_context(tc.tile_pool(name="outs", bufs=4))
        psum = ctx.enter_context(tc.psum_pool(name="psum", bufs=8))

        wd_raw = keep.tile([P, PASSES, PACK, R], BF16, align_bytes=64)
        x_raw = keep.tile([P, TILES, C], BF16, align_bytes=64)
        scale = keep.tile([P, PACK], F32)
        freqs = keep.tile([P, T // P, HALF, 2], BF16)
        wk_raw = []
        wv_raw = []
        for u in range(UNITS):
            raw_k = keep.tile([P, PACK, UW], U8, name="wk_raw%d" % u, align_bytes=64)
            wk_raw.append(raw_k)
        for c in range(H * DV // BANK):
            raw_v = keep.tile([P, PACK, BANK], BF16, name="wv_raw%d" % c, align_bytes=64)
            wv_raw.append(raw_v)
        wd_view = w_kv_down.rearrange("(g p j) n -> g p j n", p=P, j=PACK)
        wk_view = w_k_up_bytes.rearrange("(p j) n -> p j n", j=PACK)
        wv_view = w_v_up.rearrange("(p j) n -> p j n", j=PACK)

        def load_wd(g):
            nc.sync.dma_start(out=wd_raw[:, g], in_=wd_view[g])

        def load_x(i):
            nc.sync.dma_start(out=x_raw[:, i], in_=x_rows[i * P : (i + 1) * P, :])

        def load_wk(u):
            nc.sync.dma_start(out=wk_raw[u][:], in_=wk_view[:, :, u * UW : (u + 1) * UW])

        def load_wka(j):
            nc.sync.dma_start(out=wk_raw[0][:, j, :], in_=wk_view[:, j, 0:UW])

        def load_wv(c):
            cols = slice(c * BANK, (c + 1) * BANK)
            nc.sync.dma_start(out=wv_raw[c][:], in_=wv_view[:, :, cols])

        load_wd(1)
        load_wv(0)
        load_wd(0)
        load_wka(0)
        load_wka(3)
        nc.sync.dma_start(out=scale[:], in_=w_k_up_scale.rearrange("(p j) o -> p (j o)", j=PACK))
        load_x(0)
        load_wd(2)
        load_wka(1)
        load_wka(2)
        load_x(1)
        load_wd(3)
        load_x(3)
        load_wk(1)
        load_x(2)
        load_wv(1)
        nc.sync.dma_start(out=freqs[:], in_=freqs_cis.rearrange("(a p) f c -> p a f c", p=P))
        load_wv(2)
        load_wv(3)

        ident_f = keep.tile([P, P], F32)
        ident_b = keep.tile([P, P], BF16)
        make_identity(nc, ident_b[:])
        make_identity(nc, ident_f[:])
        warm = keep.tile([P, 1], F32)
        nc.vector.memset(warm[:], 0.0)
        warm2 = keep.tile([P, 1], F32)
        nc.scalar.activation(out=warm2[:], in_=warm[:], func=COPY)
        cs = keep.tile([P, T // P, 2, HALF], F32)
        sc = keep.tile([P, T // P, 2, HALF], F32)
        nc.gpsimd.tensor_copy(out=cs[:, :, 0, :], in_=freqs[:, :, :, 0])
        nc.gpsimd.tensor_copy(out=cs[:, :, 1, :], in_=freqs[:, :, :, 1])
        nc.gpsimd.tensor_scalar(out=sc[:, :, 0, :], in0=freqs[:, :, :, 1], scalar1=-1.0, scalar2=None, op0=MULT)
        nc.gpsimd.tensor_copy(out=sc[:, :, 1, :], in_=freqs[:, :, :, 0])

        wd_codes = keep.tile([P, PASSES, R], U32, align_bytes=64)
        wd_scales = keep.tile([P, PASSES, R], U8, align_bytes=64)
        x_codes = keep.tile([P, TILES, PASSES, P], U32, align_bytes=64)
        x_scales = keep.tile([P, TILES, PASSES, P], U8, align_bytes=64)
        kv_codes = keep.tile([P, TILES, P], U32, align_bytes=64)
        kv_scales = keep.tile([P, TILES, P], U8, align_bytes=64)
        wk_codes = keep.tile([P, UNITS, UW], U32, align_bytes=64)
        wk_scales = keep.tile([P, UNITS, UW], U8, align_bytes=64)
        wv_codes = keep.tile([P, VUNITS, VW], U32, align_bytes=64)
        wv_scales = keep.tile([P, VUNITS, VW], U8, align_bytes=64)

        def quantize(codes, scales, grouped):
            nc.vector.quantize_mx(out=codes.bitcast(FP8X4), scales=scales, in_=grouped)

        def mx(out, lhs, rhs, start=True, stop=True):
            nc.tensor.matmul_mx(out=out, lhsT=lhs[0].bitcast(FP8X4), lhsT_scale=lhs[1], rhs=rhs[0].bitcast(FP8X4), rhs_scale=rhs[1], start=start, stop=stop)


        live = {}

        def copy_out(engine, dst, src):
            if engine == "s":
                nc.scalar.copy(out=dst, in_=src)
            else:
                nc.vector.tensor_copy(out=dst, in_=src)

        def staged(key):
            if key not in live:
                grouped = work.tile([P, BANK * PACK], BF16, tag="grouped", align_bytes=64)
                live[key] = grouped
            return live[key]

        def wdP(g, h):
            raw = wd_raw[:, g].rearrange("p j (m t) -> p j m t", t=PACK)
            bank = psum.tile([P, 2 * BANK], BF16, tag="bank")
            dst = bank[:].rearrange("p (t m j) -> p j m t", t=2, j=PACK)
            for j in range(0, PACK, 2):
                nc.tensor.matmul(dst[:, j : j + 2], lhsT=ident_b[:], rhs=raw[:, j : j + 2, :, 2 * h : 2 * h + 2], start=True, stop=True)
            live["wd", g, h] = bank

        def wdC(g, h, engine):
            grouped = staged(("wdg", g))
            copy_out(engine, grouped[:, h * 2 * BANK : (h + 1) * 2 * BANK], live["wd", g, h][:])

        def wdQ(g):
            quantize(wd_codes[:, g, :], wd_scales[:, g, :], live["wdg", g][:])

        def xP(i, h):
            words = x_raw[:, i].bitcast(F32)
            bank = psum.tile([P, 2, 2, P], F32, tag="bank")
            for s in range(2):
                g = 2 * h + s
                for w in range(2):
                    nc.tensor.transpose(bank[:, s, w, :], words[:, 256 * g + w : 256 * (g + 1) : 2], ident_f[:])
            live["x", i, h] = bank

        def xC(i, h, engine):
            grouped = staged(("xg", i))
            dst = grouped[:, h * 2 * BANK : (h + 1) * 2 * BANK].bitcast(F32)
            copy_out(engine, dst.rearrange("p (g r w) -> p g r w", g=2, w=2), live["x", i, h][:].rearrange("p g w r -> p g r w"))

        def xQ(i):
            quantize(x_codes[:, i].rearrange("p g r -> p (g r)"), x_scales[:, i].rearrange("p g r -> p (g r)"), live["xg", i][:])

        def kvP(i):
            bank = psum.tile([P, PACK, P], F32, tag="bank")
            for t in range(PACK):
                cols = slice(t * P, (t + 1) * P)
                for g in range(PASSES):
                    mx(bank[:, t, :], (wd_codes[:, g, cols], wd_scales[:, g, cols]), (x_codes[:, i, g, :], x_scales[:, i, g, :]), start=(g == 0), stop=(g == PASSES - 1))
            live["kv", i] = bank

        def kvC(i, engine):
            grouped = work.tile([P, P, PACK], BF16, tag="kvg", align_bytes=64)
            live["kvg", i] = grouped
            copy_out(engine, grouped[:], live["kv", i][:].rearrange("p t n -> p n t"))

        def kvQ(i):
            quantize(kv_codes[:, i, :], kv_scales[:, i, :], live["kvg", i][:].rearrange("p n t -> p (n t)"))

        def wn(u, j, engine):
            wide = (wide0, wide1)[u]
            src = wk_raw[u][:, j, :].bitcast(FP8)
            if engine == "s":
                nc.scalar.activation(out=wide[:, j, :], in_=src, func=COPY, scale=scale[:, j : j + 1])
            else:
                nc.vector.tensor_scalar(out=wide[:, j, :], in0=src, scalar1=scale[:, j : j + 1], scalar2=None, op0=MULT)

        PARTS = ((0, 4, DN, 0), (0, 8, DR, DN), (4, 4, DN, 0))

        def il(u, part):
            wide = (wide0, wide1)[u]
            first, heads, width, offset = PARTS[part]
            grouped = staged(("wkg", u, part))
            src = wide[:].rearrange("p j (h c) -> p h c j", c=DQ)[:, first : first + heads, offset : offset + width, :]
            if part == 1:
                nc.vector.tensor_copy(out=grouped[:].rearrange("p (h c j) -> p h c j", h=heads, j=PACK), in_=src)
            else:
                nc.vector.tensor_copy(
                    out=grouped[:].rearrange("p (h c i j) -> p h c j i", h=heads, i=4, j=PACK),
                    in_=src.rearrange("p h (c i) j -> p h c j i", i=4),
                )

        def iq(u, part):
            base = (0, UN, BANK)[part]
            quantize(wk_codes[:, u, base : base + BANK], wk_scales[:, u, base : base + BANK], live["wkg", u, part][:])

        def kv_lhs(i):
            return (kv_codes[:, i, :], kv_scales[:, i, :])

        def kout(u, i):
            if ("ko", u, i) not in live:
                o = outs.tile([P, UH, DQ], F32, tag="ko", bufs=6, align_bytes=64)
                live["ko", u, i] = o
            return live["ko", u, i]

        def kR(u, i):
            rope = psum.tile([P, UH, 2, HALF], F32, tag="bank")
            mx(rope[:].rearrange("p h e c -> p (h e c)"), kv_lhs(i), (wk_codes[:, u, UN:UW], wk_scales[:, u, UN:UW]))
            live["rope", u, i] = rope

        def rope_product(u, i, e, table):
            full = [P, UH, 2, HALF]
            a = i % (T // P)
            prod = outs.tile([P, UH, 2, HALF], F32, name="prod%d" % e, align_bytes=64)
            nc.vector.tensor_tensor(out=prod[:], in0=live["rope", u, i][:, :, e : e + 1, :].to_broadcast(full), in1=table[:, a : a + 1].to_broadcast(full), op=MULT)
            live["prod", u, i, e] = prod

        def kA(u, i):
            rope_product(u, i, 0, cs)

        def kB(u, i):
            rope_product(u, i, 1, sc)

        def kG(u, i, engine="g"):
            a, b = (live["prod", u, i, e][:].rearrange("p h e c -> p h (e c)") for e in range(2))
            o = kout(u, i)
            if engine == "g":
                nc.gpsimd.tensor_tensor(out=o[:, :, DN:DQ], in0=a, in1=b, op=ADD)
            else:
                nc.vector.tensor_tensor(out=o[:, :, DN:DQ], in0=a, in1=b, op=ADD)

        def kN(u, i, n):
            cols = slice(n * BANK, (n + 1) * BANK)
            bank = psum.tile([P, BANK], F32, tag="bank")
            mx(bank[:], kv_lhs(i), (wk_codes[:, u, cols], wk_scales[:, u, cols]))
            live["nope", u, i, n] = bank

        def kC(u, i, n, engine):
            hs = BANK // DN
            copy_out(engine, kout(u, i)[:, n * hs : (n + 1) * hs, 0:DN], live["nope", u, i, n][:].rearrange("p (h c) -> p h c", c=DN))

        def storeK(u, i, n):
            hs = UH // 2
            c0 = u * UW + n * hs * DQ
            nc.sync.dma_start(out=k_rows[i * P : (i + 1) * P, c0 : c0 + hs * DQ], in_=live["ko", u, i][:, n * hs : (n + 1) * hs, :].rearrange("p h d -> p (h d)"))

        def vI(c, h):
            grouped = staged(("wvg", c))
            c0 = h * 256
            src = wv_raw[c][:, :, c0 : c0 + 256]
            dst = grouped[:, h * 1024 : (h + 1) * 1024]
            nc.vector.tensor_copy(out=dst.rearrange("p (c i j) -> p c j i", i=4, j=PACK), in_=src.rearrange("p j (c i) -> p c j i", i=4))

        def vP(c, h):
            bank = psum.tile([P, 2 * BANK], BF16, tag="bank")
            dst = bank[:].rearrange("p (c j) -> p j c", j=PACK)
            for j in range(0, PACK, 2):
                nc.tensor.matmul(dst[:, j : j + 2], lhsT=ident_b[:], rhs=wv_raw[c][:, j : j + 2, h * 256 : (h + 1) * 256], start=True, stop=True)
            live["wv", c, h] = bank

        def vC(c, h, engine):
            grouped = staged(("wvg", c))
            copy_out(engine, grouped[:, h * 1024 : (h + 1) * 1024], live["wv", c, h][:])

        def vQ(c):
            cols = slice((c % 2) * BANK, (c % 2 + 1) * BANK)
            quantize(wv_codes[:, c // 2, cols], wv_scales[:, c // 2, cols], live["wvg", c][:])

        def vM(c, i):
            cols = slice((c % 2) * BANK, (c % 2 + 1) * BANK)
            bank = psum.tile([P, BANK], F32, tag="bank")
            mx(bank[:], kv_lhs(i), (wv_codes[:, c // 2, cols], wv_scales[:, c // 2, cols]))
            live["vo", c, i] = bank

        def vX(c, i, engine):
            o = outs.tile([P, BANK], F32, tag="vo", bufs=8, align_bytes=64)
            copy_out(engine, o[:], live["vo", c, i][:])
            live["vs", c, i] = o

        def storeV(c, i):
            nc.sync.dma_start(out=v_rows[i * P : (i + 1) * P, c * BANK : (c + 1) * BANK], in_=live["vs", c, i][:])

        wide0 = keep.tile([P, PACK, UW], BF16, align_bytes=64)
        wide1 = keep.tile([P, PACK, UW], BF16, align_bytes=64)
        ctx.enter_context(tc.manual_schedule())
        wdP(1, 0)
        wdP(1, 1)
        wdC(1, 1, "s")
        wdC(1, 0, "v")
        vI(0, 0)
        vI(0, 1)
        wdP(0, 1)
        wn(0, 3, "v")
        wdP(0, 0)
        xP(0, 1)
        xP(0, 0)
        wdC(0, 1, "s")
        vQ(0)
        wdP(2, 1)
        wdP(2, 0)
        xP(1, 1)
        wdC(0, 0, "v")
        wn(0, 0, "s")
        wn(0, 1, "s")
        wdQ(1)
        xP(1, 0)
        xC(0, 0, "s")
        xC(0, 1, "s")
        wdQ(0)
        xC(1, 1, "s")
        wn(0, 2, "v")
        il(0, 2)
        xQ(0)
        xC(1, 0, "s")
        wdC(2, 0, "s")
        iq(0, 2)
        wdP(3, 0)
        wdC(2, 1, "s")
        xQ(1)
        wdP(3, 1)
        xP(3, 0)
        wdC(3, 0, "s")
        wdC(3, 1, "s")
        wn(1, 3, "s")
        il(0, 0)
        wdQ(2)
        xP(3, 1)
        xC(3, 1, "s")
        wdQ(3)
        xP(2, 1)
        iq(0, 0)
        il(0, 1)
        kvP(1)
        kvP(0)
        xC(3, 0, "s")
        kvC(1, "s")
        xQ(3)
        kvP(3)
        iq(0, 1)
        xC(2, 1, "s")
        kvQ(1)
        wn(1, 1, "s")
        kvC(3, "s")
        vM(0, 1)
        vI(1, 0)
        xP(2, 0)
        kN(0, 1, 0)
        kN(0, 1, 1)
        kvC(0, "s")
        wn(1, 2, "v")
        vI(1, 1)
        kvQ(3)
        vI(3, 1)
        vM(0, 3)
        vX(0, 1, "s")
        kvQ(0)
        kR(0, 1)
        vX(0, 3, "s")
        vQ(1)
        xC(2, 0, "s")
        vM(0, 0)
        storeV(0, 1)
        vP(3, 0)
        kA(0, 1)
        kC(0, 1, 0, "s")
        vM(1, 0)
        vX(0, 0, "v")
        kC(0, 1, 1, "s")
        kR(0, 0)
        storeV(0, 3)
        kB(0, 1)
        vM(1, 1)
        kA(0, 0)
        vX(1, 0, "s")
        vM(1, 3)
        vX(1, 1, "s")
        vX(1, 3, "v")
        kG(0, 1)
        kB(0, 0)
        kN(0, 0, 1)
        vP(2, 1)
        kR(0, 3)
        vC(3, 0, "s")
        vQ(3)
        storeV(0, 0)
        storeV(1, 0)
        xQ(2)
        storeV(1, 1)
        kA(0, 3)
        storeV(1, 3)
        kN(0, 0, 0)
        vC(2, 1, "v")
        kC(0, 0, 1, "s")
        kG(0, 0)
        vP(2, 0)
        storeK(0, 1, 0)
        vM(3, 0)
        storeK(0, 1, 1)
        wn(1, 0, "s")
        vC(2, 0, "s")
        kB(0, 3)
        vQ(2)
        storeK(0, 0, 1)
        kvP(2)
        vM(3, 3)
        il(1, 2)
        kC(0, 0, 0, "s")
        vX(3, 0, "s")
        kvC(2, "s")
        vX(3, 3, "s")
        vM(3, 1)
        vX(3, 1, "s")
        vM(2, 1)
        kvQ(2)
        storeK(0, 0, 0)
        vM(2, 0)
        kR(0, 2)
        vX(2, 1, "s")
        il(1, 1)
        vX(2, 0, "s")
        vM(1, 2)
        vM(3, 2)
        vM(0, 2)
        storeV(3, 0)
        storeV(3, 3)
        vX(1, 2, "s")
        kN(0, 3, 1)
        kA(0, 2)
        kG(0, 3)
        vM(2, 2)
        kN(0, 3, 0)
        vX(2, 2, "s")
        vM(2, 3)
        vX(0, 2, "s")
        kB(0, 2)
        kC(0, 3, 1, "s")
        kN(0, 2, 0)
        storeV(3, 1)
        kC(0, 3, 0, "s")
        kC(0, 2, 0, "s")
        iq(1, 1)
        vX(3, 2, "s")
        storeV(2, 1)
        iq(1, 2)
        storeV(2, 0)
        kR(1, 2)
        kN(0, 2, 1)
        il(1, 0)
        storeV(1, 2)
        vX(2, 3, "s")
        kA(1, 2)
        storeV(2, 2)
        storeV(0, 2)
        kN(1, 2, 1)
        kN(1, 1, 1)
        kR(1, 1)
        kC(1, 2, 1, "s")
        kG(0, 2)
        kB(1, 2)
        iq(1, 0)
        storeK(0, 3, 1)
        kC(0, 2, 1, "s")
        kR(1, 3)
        kC(1, 1, 1, "s")
        storeK(0, 3, 0)
        storeV(3, 2)
        kA(1, 1)
        kN(1, 3, 1)
        kB(1, 1)
        kA(1, 3)
        kC(1, 3, 1, "s")
        kN(1, 2, 0)
        kG(1, 2)
        storeV(2, 3)
        kR(1, 0)
        kG(1, 1)
        kC(1, 2, 0, "s")
        kN(1, 0, 0)
        kN(1, 3, 0)
        storeK(0, 2, 0)
        kB(1, 3)
        kN(1, 0, 1)
        storeK(0, 2, 1)
        kC(1, 3, 0, "s")
        kN(1, 1, 0)
        storeK(1, 2, 1)
        kC(1, 0, 0, "v")
        storeK(1, 2, 0)
        kA(1, 0)
        storeK(1, 1, 1)
        kC(1, 1, 0, "s")
        storeK(1, 1, 0)
        kB(1, 0)
        kG(1, 3)
        storeK(1, 3, 1)
        kC(1, 0, 1, "s")
        kG(1, 0)
        storeK(1, 3, 0)
        storeK(1, 0, 0)
        storeK(1, 0, 1)
